import numpy as np
import ml_dtypes


def mxq(x, axis, fmt="e4m3"):
    dtype, down = {"e4m3": (ml_dtypes.float8_e4m3fn, 7), "e5m2": (ml_dtypes.float8_e5m2, 14)}[fmt]
    v = np.moveaxis(np.asarray(x, np.float32).astype(ml_dtypes.bfloat16).astype(np.float64), axis, -1)
    blocks = v.reshape(v.shape[:-1] + (-1, 32))
    amax = np.abs(blocks).max(-1, keepdims=True)
    byte = np.maximum(np.where(amax > 0, np.frexp(amax)[1] - 1 + 127, 0) - down, 1)
    scale = np.exp2(byte - 127.0)
    codes = (blocks / scale).astype(np.float32).astype(dtype).astype(np.float64)
    return np.moveaxis((codes * scale).reshape(v.shape), -1, axis)


WIDE = False


def mx_kscale(k):
    if not WIDE:
        return np.ones(k)
    levels = np.array([20, -20, 10, -10, 0])
    a = np.random.permutation(np.resize(levels, k // 512 * 4)).reshape(k // 512, 4)
    idx = np.arange(k)
    return np.exp2(a[idx // 512, idx % 128 // 32])


BF16 = ml_dtypes.bfloat16


def bf(x):
    return np.asarray(x, np.float32).astype(BF16)


def f64(x):
    return np.asarray(x).astype(np.float64)


B, C, H, W, KS, CO = 1, 32, 131, 131, 4, 512
OH, OW = H - KS + 1, W - KS + 1
Q = C * KS * KS
T = B * OH * OW
TPC = OH * OW // C


def unfold_patches(x, k):
    oh, ow = x.shape[2] - k + 1, x.shape[3] - k + 1
    rows = []
    for di in range(k):
        cols = [x[:, :, di:di + oh, dj:dj + ow] for dj in range(k)]
        rows.append(np.stack(cols, axis=-1))
    return np.stack(rows, axis=-2)


def wide_factors():
    s = mx_kscale(T).reshape(B, C, TPC)[:, :, 0]
    return s[:, :, None, None], np.repeat(s.reshape(-1), TPC).reshape(B, 1, OH, OW)


def setup_inputs():
    fx, fg = wide_factors()
    x = np.random.standard_normal((B, C, H, W)) * fx
    weights = np.random.standard_normal((Q, CO)) / np.sqrt(Q)
    bias = np.random.standard_normal(CO) * 0.3
    g = np.random.standard_normal((B, CO, OH, OW)) * np.exp2(np.random.randint(-12, 1, (B, 1, OH, OW))) * 0.25 / fg
    return {"x": bf(x), "weights": bf(weights), "bias": bf(bias), "grad_out": bf(g)}


def reference(x, weights, bias, grad_out):
    a = unfold_patches(f64(x), KS).reshape(T, Q)
    g = np.transpose(f64(grad_out), (0, 2, 3, 1)).reshape(T, CO)
    return mxq(a, 0, "e4m3").T @ mxq(g, 0, "e5m2")

@@ -1,0 +1,232 @@
+from contextlib import ExitStack
+
+import concourse.mybir as mybir
+from concourse.masks import make_identity
+
+BF16 = mybir.dt.bfloat16
+F32 = mybir.dt.float32
+I32 = mybir.dt.int32
+U32 = mybir.dt.uint32
+U8 = mybir.dt.uint8
+E4M3X4 = mybir.dt.float8_e4m3fn_x4
+E5M2X4 = mybir.dt.float8_e5m2_x4
+
+P = 128
+C = 32
+HW = 131
+KS = 4
+CO = 512
+TOK = 512
+RUN = KS * HW
+XCH = 4
+NXC = C // XCH
+ESLOT = 64
+G_CHUNKS = ((0, 1), (1, 1), (2, 2), (4, 4), (8, 4), (12, 4), (16, 4), (20, 4), (24, 4), (28, 4))
+G_BUFS = 6
+X_BUFS = 4
+FLOPS = 2 * C * TOK * 512 * CO
+
+
+def tile_conv2d_kernel(tc, x, weights, bias, grad_out, out):
+    nc = tc.nc
+    with ExitStack() as ctx:
+        keep = ctx.enter_context(tc.tile_pool(name="keep", bufs=1))
+        gpool = ctx.enter_context(tc.tile_pool(name="gload", bufs=G_BUFS))
+        xpool = ctx.enter_context(tc.tile_pool(name="xload", bufs=X_BUFS))
+        apool = ctx.enter_context(tc.tile_pool(name="agroup", bufs=2))
+        qpool = ctx.enter_context(tc.tile_pool(name="ggroup", bufs=4))
+        cpool = ctx.enter_context(tc.tile_pool(name="gcodes", bufs=4))
+        psum_t = ctx.enter_context(tc.psum_pool(name="psum_t", bufs=6))
+        psum_r = ctx.enter_context(tc.psum_pool(name="psum_r", bufs=1))
+        ctx.enter_context(tc.manual_schedule())
+
+        x_v = x.rearrange("n c y z -> (n c) y z")
+        g_v = grad_out.rearrange("n (j p) u v -> p (n j) (u v)", p=P)
+        out_v = out.rearrange("(m j) o -> j m o", j=KS)
+
+        ident = keep.tile([P, P], F32, name="ident")
+        a_codes = keep.tile([P, C * P], U32, name="a_codes", align_bytes=64)
+        a_scales = keep.tile([P, C * P], U8, name="a_scales", align_bytes=64)
+        e_codes = keep.tile([P, (C + 1) * ESLOT], U32, name="e_codes", align_bytes=64)
+        e_scales = keep.tile([P, (C + 1) * ESLOT], U8, name="e_scales", align_bytes=64)
+        e_in = [
+            keep.tile([P, XCH * ESLOT * 4], BF16, name="e_in%d" % i, align_bytes=64)
+            for i in range(2)
+        ]
+        r_main = psum_r.tile([P, CO], F32, name="r_main")
+        r_extra = psum_r.tile([P, CO], F32, name="r_extra")
+
+        for i in range(2):
+            nc.vector.memset(e_in[i][:].bitcast(I32), 0)
+        nc.vector.memset(e_codes[:, C * ESLOT :].bitcast(I32), 0)
+        nc.vector.memset(e_scales[:, C * ESLOT :].bitcast(I32), 0)
+        make_identity(nc, ident[:])
+
+        g_tiles = {}
+        x_tiles = {}
+        state = {"next": 0, "t_done": 0, "x_done": 0}
+        plan = [("g", 0), ("x", 0), ("g", 1), ("g", 2)]
+        for k in range(1, NXC):
+            plan.append(("x", k))
+            plan.append(("g", k + 2))
+
+        def load_g(i):
+            c0, n = G_CHUNKS[i]
+            gt = gpool.tile([P, 4 * n * TOK], BF16, name="gt", tag="gt")
+            nc.sync.dma_start(
+                out=gt[:].rearrange("p (j r) -> p j r", j=4),
+                in_=g_v[:, :, c0 * TOK : (c0 + n) * TOK],
+            )
+            g_tiles[i] = gt
+
+        def load_x(k):
+            xt = xpool.tile([P, XCH * RUN], BF16, name="xt", tag="xt")
+            for b in range(KS):
+                nc.sync.dma_start(
+                    out=xt[b:P:KS, :].rearrange("a (c w) -> a c w", c=XCH),
+                    in_=x_v[k * XCH : (k + 1) * XCH, b : b + P, :].rearrange(
+                        "c (a r) z -> a c (r z)", r=KS
+                    ),
+                )
+            x_tiles[k] = xt
+
+        def pump():
+            while state["next"] < len(plan):
+                kind, i = plan[state["next"]]
+                if kind == "g" and i >= G_BUFS and state["t_done"] < sum(G_CHUNKS[i - G_BUFS]):
+                    return
+                if kind == "x" and i >= X_BUFS and state["x_done"] < i - X_BUFS + 1:
+                    return
+                if kind == "g":
+                    load_g(i)
+                else:
+                    load_x(i)
+                state["next"] = state["next"] + 1
+
+        a_in = {}
+
+        def regroup(k):
+            xt = x_tiles[k]
+            rows = xt[:].rearrange("p (c d z) -> p c d z", c=XCH, d=KS)
+            at = apool.tile([P, XCH * P * 4], BF16, name="at", tag="at", align_bytes=64)
+            dst = at[:].rearrange("p (c s d t) -> p c s d t", c=XCH, d=KS, t=4)
+            for d in range(KS):
+                nc.vector.tensor_copy(
+                    out=dst[:, :, :, d, :],
+                    in_=rows[:, :, d, 0:P].rearrange("p c (t s) -> p c s t", t=4),
+                )
+            edst = e_in[k % 2][:].rearrange("p (c s d t) -> p c s d t", c=XCH, d=KS, t=4)
+            for s in range(KS - 1):
+                nc.scalar.copy(out=edst[:, :, s, :, :], in_=rows[:, :, :, 32 + s : HW : 32])
+            a_in[k] = at
+            state["x_done"] = k + 1
+
+        def quantise_a(k):
+            w = XCH * P
+            nc.vector.quantize_mx(
+                out=a_codes[:, k * w : (k + 1) * w].bitcast(E4M3X4),
+                scales=a_scales[:, k * w : (k + 1) * w],
+                in_=a_in[k][:],
+            )
+            w = XCH * ESLOT
+            nc.vector.quantize_mx(
+                out=e_codes[:, k * w : (k + 1) * w].bitcast(E4M3X4),
+                scales=e_scales[:, k * w : (k + 1) * w],
+                in_=e_in[k % 2][:],
+            )
+
+        chunk_of = {}
+        for i, (c0, n) in enumerate(G_CHUNKS):
+            for c in range(c0, c0 + n):
+                chunk_of[c] = i
+
+        grouped = {}
+
+        def transpose_and_copy(c):
+            i = chunk_of[c]
+            c0, n = G_CHUNKS[i]
+            words = g_tiles[i][:].bitcast(F32)
+            gq = qpool.tile([P, CO * 4], BF16, name="gq", tag="gq", align_bytes=64)
+            gq_words = gq[:].bitcast(F32)
+            banks = []
+            for h in range(2):
+                pt = psum_t.tile([P, 2, 256], F32, name="pt", tag="pt")
+                for jj in range(2):
+                    base = ((2 * h + jj) * n + (c - c0)) * (TOK // 2)
+                    for u in range(2):
+                        nc.tensor.transpose(
+                            out=pt[:, u, jj * P : (jj + 1) * P],
+                            in_=words[:, base + u : base + TOK // 2 : 2],
+                            identity=ident[:],
+                        )
+                banks.append(pt)
+            for h in range(2):
+                nc.scalar.copy(
+                    out=gq_words[:, h * 512 : (h + 1) * 512].rearrange("p (o u) -> p o u", u=2),
+                    in_=banks[h][:].rearrange("p u o -> p o u"),
+                )
+            grouped[c] = gq
+            state["t_done"] = c + 1
+
+        g_q = {}
+
+        def quantise_g(c):
+            gc = cpool.tile([P, CO], U32, name="gc", tag="gc", align_bytes=64)
+            gs = cpool.tile([P, CO], U8, name="gs", tag="gs", align_bytes=64)
+            nc.vector.quantize_mx(out=gc[:].bitcast(E5M2X4), scales=gs[:], in_=grouped[c][:])
+            g_q[c] = (gc, gs)
+
+        def multiply(c):
+            gc, gs = g_q[c]
+            nc.tensor.matmul_mx(
+                out=r_main[:],
+                lhsT=a_codes[:, c * P : (c + 1) * P].bitcast(E4M3X4),
+                lhsT_scale=a_scales[:, c * P : (c + 1) * P],
+                rhs=gc[:].bitcast(E5M2X4),
+                rhs_scale=gs[:],
+                start=(c == 0),
+                stop=(c == C - 1),
+            )
+            nc.tensor.matmul_mx(
+                out=r_extra[:],
+                lhsT=e_codes[:, c * ESLOT : c * ESLOT + P].bitcast(E4M3X4),
+                lhsT_scale=e_scales[:, c * ESLOT : c * ESLOT + P],
+                rhs=gc[:].bitcast(E5M2X4),
+                rhs_scale=gs[:],
+                start=(c == 0),
+                stop=(c == C - 1),
+            )
+
+        n_groups = C // 2
+        pump()
+        regroup(0)
+        pump()
+        quantise_a(0)
+        for g in range(n_groups + 1):
+            if g < n_groups:
+                transpose_and_copy(2 * g)
+                transpose_and_copy(2 * g + 1)
+                pump()
+            if g % 2 == 1 and (g + 1) // 2 < NXC:
+                regroup((g + 1) // 2)
+                pump()
+            if g % 2 == 0 and 0 < g // 2 < NXC:
+                quantise_a(g // 2)
+            if g > 0:
+                quantise_g(2 * g - 2)
+                quantise_g(2 * g - 1)
+                multiply(2 * g - 2)
+                multiply(2 * g - 1)
+
+        main_sb = keep.tile([P, CO], F32, name="main_sb")
+        extra_sb = keep.tile([P, CO], F32, name="extra_sb")
+        nc.vector.tensor_copy(out=main_sb[:], in_=r_main[:])
+        nc.scalar.copy(out=extra_sb[0:16, :], in_=r_extra[0:16, :])
+        nc.sync.dma_start(out=out_v[0, :, :], in_=main_sb[:, :])
+        nc.scalar.dma_start(out=out_v[2, 8:120, :], in_=main_sb[16:P, :])
+        nc.sync.dma_start(out=out_v[1, 12:124, :], in_=main_sb[16:P, :])
+        nc.scalar.dma_start(out=out_v[3, 4:116, :], in_=main_sb[16:P, :])
+        for j in range(1, KS):
+            eng = nc.sync if j % 2 == 1 else nc.scalar
+            eng.dma_start(out=out_v[j, 0 : 16 - 4 * j, :], in_=main_sb[4 * j : 16, :])
+            eng.dma_start(out=out_v[j, P - 4 * j : P, :], in_=extra_sb[0 : 4 * j, :])

@@ -24,6 +24,7 @@ ESLOT = 64
 G_CHUNKS = ((0, 1), (1, 1), (2, 2), (4, 4), (8, 4), (12, 4), (16, 4), (20, 4), (24, 4), (28, 4))
 G_BUFS = 6
 X_BUFS = 4
+SORTER = ("", "v", "s", "v", "", "s", "", "v")
 FLOPS = 2 * C * TOK * 512 * CO
 
 
@@ -36,6 +37,7 @@ def tile_conv2d_kernel(tc, x, weights, bias, grad_out, out):
         apool = ctx.enter_context(tc.tile_pool(name="agroup", bufs=2))
         qpool = ctx.enter_context(tc.tile_pool(name="ggroup", bufs=4))
         cpool = ctx.enter_context(tc.tile_pool(name="gcodes", bufs=4))
+        spool = ctx.enter_context(tc.tile_pool(name="gsort", bufs=4))
         psum_t = ctx.enter_context(tc.psum_pool(name="psum_t", bufs=6))
         psum_r = ctx.enter_context(tc.psum_pool(name="psum_r", bufs=1))
         ctx.enter_context(tc.manual_schedule())
@@ -73,10 +75,11 @@ def tile_conv2d_kernel(tc, x, weights, bias, grad_out, out):
         def load_g(i):
             c0, n = G_CHUNKS[i]
             gt = gpool.tile([P, 4 * n * TOK], BF16, name="gt", tag="gt")
-            nc.sync.dma_start(
-                out=gt[:].rearrange("p (j r) -> p j r", j=4),
-                in_=g_v[:, :, c0 * TOK : (c0 + n) * TOK],
-            )
+            dst = gt[:].rearrange("p (j r) -> p j r", j=4)
+            for j0, j1 in ((0, 2), (2, 4)) if i == 0 else ((0, 4),):
+                nc.sync.dma_start(
+                    out=dst[:, j0:j1, :], in_=g_v[:, j0:j1, c0 * TOK : (c0 + n) * TOK]
+                )
             g_tiles[i] = gt
 
         def load_x(k):
@@ -141,6 +144,26 @@ def tile_conv2d_kernel(tc, x, weights, bias, grad_out, out):
                 chunk_of[c] = i
 
         grouped = {}
+        sorted_words = {}
+
+        def sorter_of(c):
+            return "" if c < 2 or c >= C - 2 else SORTER[c % 8]
+
+        def sort_words(c, engine):
+            if sorter_of(c) != engine:
+                return
+            i = chunk_of[c]
+            c0, n = G_CHUNKS[i]
+            half = TOK // 2
+            src = g_tiles[i][:].bitcast(F32).rearrange("p (j r) -> p j r", j=4)
+            src = src[:, :, (c - c0) * half : (c - c0 + 1) * half].rearrange("p j (i u) -> p j u i", u=2)
+            st = spool.tile([P, 4 * half], F32, name="st", tag="st")
+            dst = st[:].rearrange("p (j u i) -> p j u i", j=4, u=2)
+            if sorter_of(c) == "v":
+                nc.vector.tensor_copy(out=dst, in_=src)
+            else:
+                nc.scalar.copy(out=dst, in_=src)
+            sorted_words[c] = st
 
         def transpose_and_copy(c):
             i = chunk_of[c]
@@ -154,10 +177,13 @@ def tile_conv2d_kernel(tc, x, weights, bias, grad_out, out):
                 for jj in range(2):
                     base = ((2 * h + jj) * n + (c - c0)) * (TOK // 2)
                     for u in range(2):
+                        if sorter_of(c) == "":
+                            src = words[:, base + u : base + TOK // 2 : 2]
+                        else:
+                            first = ((2 * h + jj) * 2 + u) * P
+                            src = sorted_words[c][:, first : first + P]
                         nc.tensor.transpose(
-                            out=pt[:, u, jj * P : (jj + 1) * P],
-                            in_=words[:, base + u : base + TOK // 2 : 2],
-                            identity=ident[:],
+                            out=pt[:, u, jj * P : (jj + 1) * P], in_=src, identity=ident[:]
                         )
                 banks.append(pt)
             for h in range(2):
@@ -203,6 +229,9 @@ def tile_conv2d_kernel(tc, x, weights, bias, grad_out, out):
         pump()
         quantise_a(0)
         for g in range(n_groups + 1):
+            if g + 1 < n_groups:
+                sort_words(2 * g + 2, "s")
+                sort_words(2 * g + 3, "s")
             if g < n_groups:
                 transpose_and_copy(2 * g)
                 transpose_and_copy(2 * g + 1)
@@ -215,6 +244,10 @@ def tile_conv2d_kernel(tc, x, weights, bias, grad_out, out):
             if g > 0:
                 quantise_g(2 * g - 2)
                 quantise_g(2 * g - 1)
+            if g + 1 < n_groups:
+                sort_words(2 * g + 2, "v")
+                sort_words(2 * g + 3, "v")
+            if g > 0:
                 multiply(2 * g - 2)
                 multiply(2 * g - 1)
 

@@ -19,12 +19,13 @@ CO = 512
 TOK = 512
 RUN = KS * HW
 XCH = 4
-NXC = C // XCH
+X_CHUNKS = tuple((c, 4) for c in range(0, C, 4))
+PITCH = 528
 ESLOT = 64
-G_CHUNKS = ((0, 1), (1, 1), (2, 2), (4, 4), (8, 4), (12, 4), (16, 4), (20, 4), (24, 4), (28, 4))
-G_BUFS = 6
+G_CHUNKS = ((0, 1), (1, 1)) + tuple((c, 2) for c in range(2, C, 2))
+G_BUFS = 8
 X_BUFS = 4
-SORTER = ("", "v", "s", "v", "", "s", "", "v")
+SORTER = ("", "", "", "v", "", "", "", "v")
 FLOPS = 2 * C * TOK * 512 * CO
 
 
@@ -67,14 +68,21 @@ def tile_conv2d_kernel(tc, x, weights, bias, grad_out, out):
         g_tiles = {}
         x_tiles = {}
         state = {"next": 0, "t_done": 0, "x_done": 0}
-        plan = [("g", 0), ("x", 0), ("g", 1), ("g", 2)]
-        for k in range(1, NXC):
-            plan.append(("x", k))
-            plan.append(("g", k + 2))
+        x_first = dict((c0, k) for k, (c0, n) in enumerate(X_CHUNKS))
+        plan = [("g", 0), ("x", 0)]
+        for i in range(1, len(G_CHUNKS)):
+            if G_CHUNKS[i][0] in x_first:
+                plan.append(("x", x_first[G_CHUNKS[i][0]]))
+            plan.append(("g", i))
+        replaces = {}
+        for small in (True, False):
+            same = [i for i, (c0, n) in enumerate(G_CHUNKS) if (n <= 2) == small]
+            for m in range(G_BUFS, len(same)):
+                replaces[same[m]] = same[m - G_BUFS]
 
         def load_g(i):
             c0, n = G_CHUNKS[i]
-            gt = gpool.tile([P, 4 * n * TOK], BF16, name="gt", tag="gt")
+            gt = gpool.tile([P, 4 * n * TOK], BF16, name="gt", tag="gsmall" if n <= 2 else "gbig")
             dst = gt[:].rearrange("p (j r) -> p j r", j=4)
             for j0, j1 in ((0, 2), (2, 4)) if i == 0 else ((0, 4),):
                 nc.sync.dma_start(
@@ -83,11 +91,12 @@ def tile_conv2d_kernel(tc, x, weights, bias, grad_out, out):
             g_tiles[i] = gt
 
         def load_x(k):
-            xt = xpool.tile([P, XCH * RUN], BF16, name="xt", tag="xt")
+            c0, n = X_CHUNKS[k]
+            xt = xpool.tile([P, n * PITCH], BF16, name="xt", tag="xt")
             for b in range(KS):
                 nc.sync.dma_start(
-                    out=xt[b:P:KS, :].rearrange("a (c w) -> a c w", c=XCH),
-                    in_=x_v[k * XCH : (k + 1) * XCH, b : b + P, :].rearrange(
+                    out=xt[b:P:KS, :].rearrange("a (c w) -> a c w", c=n)[:, :, 0:RUN],
+                    in_=x_v[c0 : c0 + n, b : b + P, :].rearrange(
                         "c (a r) z -> a c (r z)", r=KS
                     ),
                 )
@@ -96,7 +105,7 @@ def tile_conv2d_kernel(tc, x, weights, bias, grad_out, out):
         def pump():
             while state["next"] < len(plan):
                 kind, i = plan[state["next"]]
-                if kind == "g" and i >= G_BUFS and state["t_done"] < sum(G_CHUNKS[i - G_BUFS]):
+                if kind == "g" and i in replaces and state["t_done"] < sum(G_CHUNKS[replaces[i]]):
                     return
                 if kind == "x" and i >= X_BUFS and state["x_done"] < i - X_BUFS + 1:
                     return
@@ -110,32 +119,36 @@ def tile_conv2d_kernel(tc, x, weights, bias, grad_out, out):
 
         def regroup(k):
             xt = x_tiles[k]
-            rows = xt[:].rearrange("p (c d z) -> p c d z", c=XCH, d=KS)
-            at = apool.tile([P, XCH * P * 4], BF16, name="at", tag="at", align_bytes=64)
-            dst = at[:].rearrange("p (c s d t) -> p c s d t", c=XCH, d=KS, t=4)
+            n = X_CHUNKS[k][1]
+            rows = xt[:].rearrange("p (c w) -> p c w", c=n)[:, :, 0:RUN].rearrange(
+                "p c (d z) -> p c d z", d=KS
+            )
+            at = apool.tile([P, n * P * 4], BF16, name="at", tag="at", align_bytes=64)
+            dst = at[:].rearrange("p (c s d t) -> p c s d t", c=n, d=KS, t=4)
             for d in range(KS):
                 nc.vector.tensor_copy(
                     out=dst[:, :, :, d, :],
                     in_=rows[:, :, d, 0:P].rearrange("p c (t s) -> p c s t", t=4),
                 )
-            edst = e_in[k % 2][:].rearrange("p (c s d t) -> p c s d t", c=XCH, d=KS, t=4)
+            edst = e_in[k % 2][:, 0 : n * ESLOT * 4].rearrange(
+                "p (c s d t) -> p c s d t", c=n, d=KS, t=4
+            )
             for s in range(KS - 1):
                 nc.scalar.copy(out=edst[:, :, s, :, :], in_=rows[:, :, :, 32 + s : HW : 32])
             a_in[k] = at
             state["x_done"] = k + 1
 
         def quantise_a(k):
-            w = XCH * P
+            c0, n = X_CHUNKS[k]
             nc.vector.quantize_mx(
-                out=a_codes[:, k * w : (k + 1) * w].bitcast(E4M3X4),
-                scales=a_scales[:, k * w : (k + 1) * w],
+                out=a_codes[:, c0 * P : (c0 + n) * P].bitcast(E4M3X4),
+                scales=a_scales[:, c0 * P : (c0 + n) * P],
                 in_=a_in[k][:],
             )
-            w = XCH * ESLOT
             nc.vector.quantize_mx(
-                out=e_codes[:, k * w : (k + 1) * w].bitcast(E4M3X4),
-                scales=e_scales[:, k * w : (k + 1) * w],
-                in_=e_in[k % 2][:],
+                out=e_codes[:, c0 * ESLOT : (c0 + n) * ESLOT].bitcast(E4M3X4),
+                scales=e_scales[:, c0 * ESLOT : (c0 + n) * ESLOT],
+                in_=e_in[k % 2][:, 0 : n * ESLOT * 4],
             )
 
         chunk_of = {}
@@ -147,7 +160,7 @@ def tile_conv2d_kernel(tc, x, weights, bias, grad_out, out):
         sorted_words = {}
 
         def sorter_of(c):
-            return "" if c < 2 or c >= C - 2 else SORTER[c % 8]
+            return "" if c < 12 or c >= C - 2 else SORTER[c % 8]
 
         def sort_words(c, engine):
             if sorter_of(c) != engine:
@@ -236,14 +249,14 @@ def tile_conv2d_kernel(tc, x, weights, bias, grad_out, out):
                 transpose_and_copy(2 * g)
                 transpose_and_copy(2 * g + 1)
                 pump()
-            if g % 2 == 1 and (g + 1) // 2 < NXC:
-                regroup((g + 1) // 2)
-                pump()
-            if g % 2 == 0 and 0 < g // 2 < NXC:
-                quantise_a(g // 2)
             if g > 0:
                 quantise_g(2 * g - 2)
                 quantise_g(2 * g - 1)
+            if g > 0 and 2 * g in x_first:
+                quantise_a(x_first[2 * g])
+            if 2 * g + 2 in x_first:
+                regroup(x_first[2 * g + 2])
+                pump()
             if g + 1 < n_groups:
                 sort_words(2 * g + 2, "v")
                 sort_words(2 * g + 3, "v")

@@ -17,28 +17,52 @@ HW = 131
 KS = 4
 CO = 512
 TOK = 512
+WORDS = TOK // 2
 RUN = KS * HW
-XCH = 4
-X_CHUNKS = tuple((c, 4) for c in range(0, C, 4))
 PITCH = 528
+XCH = 4
+NXC = C // XCH
 ESLOT = 64
-G_CHUNKS = ((0, 1), (1, 1)) + tuple((c, 2) for c in range(2, C, 2))
-G_BUFS = 8
+G_BUFS = 9
 X_BUFS = 4
-SORTER = ("", "", "", "v", "", "", "", "v")
 FLOPS = 2 * C * TOK * 512 * CO
+
+
+def pair_unit(c):
+    return ((c, 0), (c, 1), (c + 1, 0), (c + 1, 1))
+
+
+def g_plan():
+    pieces = [(0, 1, 0, 1), (0, 1, 1, 1), (1, 1, 0, 2)]
+    units = [pair_unit(0)]
+    for c in (2, 4, 6):
+        pieces.append((c, 2, 0, 2))
+        units.append(pair_unit(c))
+    for c in range(8, 28, 4):
+        for h in range(2):
+            pieces.append((c, 4, h, 1))
+            units.append(tuple((c + i, h) for i in range(4)))
+    for c in (28, 30):
+        pieces.append((c, 2, 0, 2))
+        units.append(pair_unit(c))
+    return pieces, units
+
+
+def is_sorted(c):
+    return (c >= 24 and c % 2 == 1) or (c >= 12 and c % 4 == 3)
 
 
 def tile_conv2d_kernel(tc, x, weights, bias, grad_out, out):
     nc = tc.nc
+    pieces, units = g_plan()
     with ExitStack() as ctx:
         keep = ctx.enter_context(tc.tile_pool(name="keep", bufs=1))
         gpool = ctx.enter_context(tc.tile_pool(name="gload", bufs=G_BUFS))
         xpool = ctx.enter_context(tc.tile_pool(name="xload", bufs=X_BUFS))
         apool = ctx.enter_context(tc.tile_pool(name="agroup", bufs=2))
-        qpool = ctx.enter_context(tc.tile_pool(name="ggroup", bufs=4))
-        cpool = ctx.enter_context(tc.tile_pool(name="gcodes", bufs=4))
-        spool = ctx.enter_context(tc.tile_pool(name="gsort", bufs=4))
+        qpool = ctx.enter_context(tc.tile_pool(name="ggroup", bufs=8))
+        cpool = ctx.enter_context(tc.tile_pool(name="gcodes", bufs=8))
+        spool = ctx.enter_context(tc.tile_pool(name="gsort", bufs=8))
         psum_t = ctx.enter_context(tc.psum_pool(name="psum_t", bufs=6))
         psum_r = ctx.enter_context(tc.psum_pool(name="psum_r", bufs=1))
         ctx.enter_context(tc.manual_schedule())
@@ -65,38 +89,43 @@ def tile_conv2d_kernel(tc, x, weights, bias, grad_out, out):
         nc.vector.memset(e_scales[:, C * ESLOT :].bitcast(I32), 0)
         make_identity(nc, ident[:])
 
+        piece_of = {}
+        for i, (c0, n, h0, nh) in enumerate(pieces):
+            for c in range(c0, c0 + n):
+                for h in range(h0, h0 + nh):
+                    piece_of[(c, h)] = i
+        last_unit = {}
+        for u, unit in enumerate(units):
+            for c, h in unit:
+                last_unit[c] = u
+
+        plan = []
+        for i, (c0, n, h0, nh) in enumerate(pieces):
+            if c0 % XCH == 0 and h0 == 0 and c0 > 0:
+                plan.append(("x", c0 // XCH))
+            plan.append(("g", i))
+            if i == 1:
+                plan.append(("x", 0))
         g_tiles = {}
         x_tiles = {}
-        state = {"next": 0, "t_done": 0, "x_done": 0}
-        x_first = dict((c0, k) for k, (c0, n) in enumerate(X_CHUNKS))
-        plan = [("g", 0), ("x", 0)]
-        for i in range(1, len(G_CHUNKS)):
-            if G_CHUNKS[i][0] in x_first:
-                plan.append(("x", x_first[G_CHUNKS[i][0]]))
-            plan.append(("g", i))
-        replaces = {}
-        for small in (True, False):
-            same = [i for i, (c0, n) in enumerate(G_CHUNKS) if (n <= 2) == small]
-            for m in range(G_BUFS, len(same)):
-                replaces[same[m]] = same[m - G_BUFS]
+        banks_left = [n * nh for (c0, n, h0, nh) in pieces]
+        state = {"next": 0, "x_done": 0}
 
         def load_g(i):
-            c0, n = G_CHUNKS[i]
-            gt = gpool.tile([P, 4 * n * TOK], BF16, name="gt", tag="gsmall" if n <= 2 else "gbig")
-            dst = gt[:].rearrange("p (j r) -> p j r", j=4)
-            for j0, j1 in ((0, 2), (2, 4)) if i == 0 else ((0, 4),):
-                nc.sync.dma_start(
-                    out=dst[:, j0:j1, :], in_=g_v[:, j0:j1, c0 * TOK : (c0 + n) * TOK]
-                )
+            c0, n, h0, nh = pieces[i]
+            gt = gpool.tile([P, 2 * nh * n * TOK], BF16, name="gt", tag="gt")
+            nc.sync.dma_start(
+                out=gt[:].rearrange("p (j r) -> p j r", j=2 * nh),
+                in_=g_v[:, 2 * h0 : 2 * (h0 + nh), c0 * TOK : (c0 + n) * TOK],
+            )
             g_tiles[i] = gt
 
         def load_x(k):
-            c0, n = X_CHUNKS[k]
-            xt = xpool.tile([P, n * PITCH], BF16, name="xt", tag="xt")
+            xt = xpool.tile([P, XCH * PITCH], BF16, name="xt", tag="xt")
             for b in range(KS):
                 nc.sync.dma_start(
-                    out=xt[b:P:KS, :].rearrange("a (c w) -> a c w", c=n)[:, :, 0:RUN],
-                    in_=x_v[c0 : c0 + n, b : b + P, :].rearrange(
+                    out=xt[b:P:KS, :].rearrange("a (c w) -> a c w", c=XCH)[:, :, 0:RUN],
+                    in_=x_v[k * XCH : (k + 1) * XCH, b : b + P, :].rearrange(
                         "c (a r) z -> a c (r z)", r=KS
                     ),
                 )
@@ -105,7 +134,7 @@ def tile_conv2d_kernel(tc, x, weights, bias, grad_out, out):
         def pump():
             while state["next"] < len(plan):
                 kind, i = plan[state["next"]]
-                if kind == "g" and i in replaces and state["t_done"] < sum(G_CHUNKS[replaces[i]]):
+                if kind == "g" and i >= G_BUFS and banks_left[i - G_BUFS] > 0:
                     return
                 if kind == "x" and i >= X_BUFS and state["x_done"] < i - X_BUFS + 1:
                     return
@@ -118,102 +147,92 @@ def tile_conv2d_kernel(tc, x, weights, bias, grad_out, out):
         a_in = {}
 
         def regroup(k):
-            xt = x_tiles[k]
-            n = X_CHUNKS[k][1]
-            rows = xt[:].rearrange("p (c w) -> p c w", c=n)[:, :, 0:RUN].rearrange(
+            rows = x_tiles[k][:].rearrange("p (c w) -> p c w", c=XCH)[:, :, 0:RUN].rearrange(
                 "p c (d z) -> p c d z", d=KS
             )
-            at = apool.tile([P, n * P * 4], BF16, name="at", tag="at", align_bytes=64)
-            dst = at[:].rearrange("p (c s d t) -> p c s d t", c=n, d=KS, t=4)
+            at = apool.tile([P, XCH * P * 4], BF16, name="at", tag="at", align_bytes=64)
+            dst = at[:].rearrange("p (c s d t) -> p c s d t", c=XCH, d=KS, t=4)
             for d in range(KS):
                 nc.vector.tensor_copy(
                     out=dst[:, :, :, d, :],
                     in_=rows[:, :, d, 0:P].rearrange("p c (t s) -> p c s t", t=4),
                 )
-            edst = e_in[k % 2][:, 0 : n * ESLOT * 4].rearrange(
-                "p (c s d t) -> p c s d t", c=n, d=KS, t=4
-            )
+            edst = e_in[k % 2][:].rearrange("p (c s d t) -> p c s d t", c=XCH, d=KS, t=4)
             for s in range(KS - 1):
                 nc.scalar.copy(out=edst[:, :, s, :, :], in_=rows[:, :, :, 32 + s : HW : 32])
             a_in[k] = at
             state["x_done"] = k + 1
 
         def quantise_a(k):
-            c0, n = X_CHUNKS[k]
+            w = XCH * P
             nc.vector.quantize_mx(
-                out=a_codes[:, c0 * P : (c0 + n) * P].bitcast(E4M3X4),
-                scales=a_scales[:, c0 * P : (c0 + n) * P],
+                out=a_codes[:, k * w : (k + 1) * w].bitcast(E4M3X4),
+                scales=a_scales[:, k * w : (k + 1) * w],
                 in_=a_in[k][:],
             )
+            w = XCH * ESLOT
             nc.vector.quantize_mx(
-                out=e_codes[:, c0 * ESLOT : (c0 + n) * ESLOT].bitcast(E4M3X4),
-                scales=e_scales[:, c0 * ESLOT : (c0 + n) * ESLOT],
-                in_=e_in[k % 2][:, 0 : n * ESLOT * 4],
+                out=e_codes[:, k * w : (k + 1) * w].bitcast(E4M3X4),
+                scales=e_scales[:, k * w : (k + 1) * w],
+                in_=e_in[k % 2][:],
             )
 
-        chunk_of = {}
-        for i, (c0, n) in enumerate(G_CHUNKS):
-            for c in range(c0, c0 + n):
-                chunk_of[c] = i
+        def bank_words(c, h):
+            i = piece_of[(c, h)]
+            c0, n, h0, nh = pieces[i]
+            words = g_tiles[i][:].bitcast(F32).rearrange("p (j r) -> p j r", j=2 * nh)
+            return words[:, 2 * (h - h0) : 2 * (h - h0) + 2, (c - c0) * WORDS : (c - c0 + 1) * WORDS]
 
-        grouped = {}
         sorted_words = {}
 
-        def sorter_of(c):
-            return "" if c < 12 or c >= C - 2 else SORTER[c % 8]
+        def sort_words(c, h):
+            st = spool.tile([P, 2 * WORDS], F32, name="st", tag="st")
+            nc.vector.tensor_copy(
+                out=st[:].rearrange("p (j u i) -> p j u i", j=2, u=2),
+                in_=bank_words(c, h).rearrange("p j (i u) -> p j u i", u=2),
+            )
+            sorted_words[(c, h)] = st
 
-        def sort_words(c, engine):
-            if sorter_of(c) != engine:
-                return
-            i = chunk_of[c]
-            c0, n = G_CHUNKS[i]
-            half = TOK // 2
-            src = g_tiles[i][:].bitcast(F32).rearrange("p (j r) -> p j r", j=4)
-            src = src[:, :, (c - c0) * half : (c - c0 + 1) * half].rearrange("p j (i u) -> p j u i", u=2)
-            st = spool.tile([P, 4 * half], F32, name="st", tag="st")
-            dst = st[:].rearrange("p (j u i) -> p j u i", j=4, u=2)
-            if sorter_of(c) == "v":
-                nc.vector.tensor_copy(out=dst, in_=src)
-            else:
-                nc.scalar.copy(out=dst, in_=src)
-            sorted_words[c] = st
+        grouped = {}
 
-        def transpose_and_copy(c):
-            i = chunk_of[c]
-            c0, n = G_CHUNKS[i]
-            words = g_tiles[i][:].bitcast(F32)
-            gq = qpool.tile([P, CO * 4], BF16, name="gq", tag="gq", align_bytes=64)
-            gq_words = gq[:].bitcast(F32)
+        def transpose_and_copy(unit):
             banks = []
-            for h in range(2):
+            for c, h in unit:
                 pt = psum_t.tile([P, 2, 256], F32, name="pt", tag="pt")
                 for jj in range(2):
-                    base = ((2 * h + jj) * n + (c - c0)) * (TOK // 2)
                     for u in range(2):
-                        if sorter_of(c) == "":
-                            src = words[:, base + u : base + TOK // 2 : 2]
+                        if is_sorted(c):
+                            first = (jj * 2 + u) * P
+                            src = sorted_words[(c, h)][:, first : first + P]
                         else:
-                            first = ((2 * h + jj) * 2 + u) * P
-                            src = sorted_words[c][:, first : first + P]
+                            src = bank_words(c, h)[:, jj, u:WORDS:2]
                         nc.tensor.transpose(
                             out=pt[:, u, jj * P : (jj + 1) * P], in_=src, identity=ident[:]
                         )
                 banks.append(pt)
-            for h in range(2):
+                banks_left[piece_of[(c, h)]] -= 1
+            for (c, h), pt in zip(unit, banks):
+                gq = qpool.tile([P, 1024], BF16, name="gq", tag="gq", align_bytes=64)
                 nc.scalar.copy(
-                    out=gq_words[:, h * 512 : (h + 1) * 512].rearrange("p (o u) -> p o u", u=2),
-                    in_=banks[h][:].rearrange("p u o -> p o u"),
+                    out=gq[:].bitcast(F32).rearrange("p (o u) -> p o u", u=2),
+                    in_=pt[:].rearrange("p u o -> p o u"),
                 )
-            grouped[c] = gq
-            state["t_done"] = c + 1
+                grouped[(c, h)] = gq
 
         g_q = {}
 
-        def quantise_g(c):
-            gc = cpool.tile([P, CO], U32, name="gc", tag="gc", align_bytes=64)
-            gs = cpool.tile([P, CO], U8, name="gs", tag="gs", align_bytes=64)
-            nc.vector.quantize_mx(out=gc[:].bitcast(E5M2X4), scales=gs[:], in_=grouped[c][:])
-            g_q[c] = (gc, gs)
+        def quantise_g(unit):
+            for c, h in unit:
+                if c not in g_q:
+                    gc = cpool.tile([P, CO], U32, name="gc", tag="gc", align_bytes=64)
+                    gs = cpool.tile([P, CO], U8, name="gs", tag="gs", align_bytes=64)
+                    g_q[c] = (gc, gs)
+                gc, gs = g_q[c]
+                nc.vector.quantize_mx(
+                    out=gc[:, h * 256 : (h + 1) * 256].bitcast(E5M2X4),
+                    scales=gs[:, h * 256 : (h + 1) * 256],
+                    in_=grouped[(c, h)][:],
+                )
 
         def multiply(c):
             gc, gs = g_q[c]
@@ -236,33 +255,37 @@ def tile_conv2d_kernel(tc, x, weights, bias, grad_out, out):
                 stop=(c == C - 1),
             )
 
-        n_groups = C // 2
         pump()
         regroup(0)
         pump()
         quantise_a(0)
-        for g in range(n_groups + 1):
-            if g + 1 < n_groups:
-                sort_words(2 * g + 2, "s")
-                sort_words(2 * g + 3, "s")
-            if g < n_groups:
-                transpose_and_copy(2 * g)
-                transpose_and_copy(2 * g + 1)
+        regrouped = 1
+        quantised = 1
+        multiplied = 0
+        u = 0
+        while multiplied < C:
+            if u < len(units):
+                transpose_and_copy(units[u])
                 pump()
-            if g > 0:
-                quantise_g(2 * g - 2)
-                quantise_g(2 * g - 1)
-            if g > 0 and 2 * g in x_first:
-                quantise_a(x_first[2 * g])
-            if 2 * g + 2 in x_first:
-                regroup(x_first[2 * g + 2])
+            if 0 < u <= len(units):
+                quantise_g(units[u - 1])
+            if quantised < regrouped and u > last_unit[quantised * XCH - 1]:
+                quantise_a(quantised)
+                quantised += 1
+            if regrouped < NXC and u >= last_unit[regrouped * XCH - 1]:
+                regroup(regrouped)
+                regrouped += 1
                 pump()
-            if g + 1 < n_groups:
-                sort_words(2 * g + 2, "v")
-                sort_words(2 * g + 3, "v")
-            if g > 0:
-                multiply(2 * g - 2)
-                multiply(2 * g - 1)
+            if u + 1 < len(units):
+                for c, h in units[u + 1]:
+                    if is_sorted(c):
+                        sort_words(c, h)
+            for i in range(2):
+                c = multiplied
+                if c < C and last_unit[c] < u and min(c + 1, C - 1) < quantised * XCH:
+                    multiply(c)
+                    multiplied += 1
+            u += 1
 
         main_sb = keep.tile([P, CO], F32, name="main_sb")
         extra_sb = keep.tile([P, CO], F32, name="extra_sb")

@@ -22,7 +22,8 @@ RUN = KS * HW
 PITCH = 528
 XCH = 4
 NXC = C // XCH
-ESLOT = 64
+ACOL = 192
+AUSED = 140
 G_BUFS = 9
 X_BUFS = 4
 FLOPS = 2 * C * TOK * 512 * CO
@@ -59,7 +60,6 @@ def tile_conv2d_kernel(tc, x, weights, bias, grad_out, out):
         keep = ctx.enter_context(tc.tile_pool(name="keep", bufs=1))
         gpool = ctx.enter_context(tc.tile_pool(name="gload", bufs=G_BUFS))
         xpool = ctx.enter_context(tc.tile_pool(name="xload", bufs=X_BUFS))
-        apool = ctx.enter_context(tc.tile_pool(name="agroup", bufs=2))
         qpool = ctx.enter_context(tc.tile_pool(name="ggroup", bufs=8))
         cpool = ctx.enter_context(tc.tile_pool(name="gcodes", bufs=8))
         spool = ctx.enter_context(tc.tile_pool(name="gsort", bufs=8))
@@ -72,21 +72,18 @@ def tile_conv2d_kernel(tc, x, weights, bias, grad_out, out):
         out_v = out.rearrange("(m j) o -> j m o", j=KS)
 
         ident = keep.tile([P, P], F32, name="ident")
-        a_codes = keep.tile([P, C * P], U32, name="a_codes", align_bytes=64)
-        a_scales = keep.tile([P, C * P], U8, name="a_scales", align_bytes=64)
-        e_codes = keep.tile([P, (C + 1) * ESLOT], U32, name="e_codes", align_bytes=64)
-        e_scales = keep.tile([P, (C + 1) * ESLOT], U8, name="e_scales", align_bytes=64)
-        e_in = [
-            keep.tile([P, XCH * ESLOT * 4], BF16, name="e_in%d" % i, align_bytes=64)
+        a_codes = keep.tile([P, C * ACOL], U32, name="a_codes", align_bytes=64)
+        a_scales = keep.tile([P, C * ACOL], U8, name="a_scales", align_bytes=64)
+        a_in = [
+            keep.tile([P, XCH * ACOL * 4], BF16, name="a_in%d" % i, align_bytes=64)
             for i in range(2)
         ]
         r_main = psum_r.tile([P, CO], F32, name="r_main")
         r_extra = psum_r.tile([P, CO], F32, name="r_extra")
 
         for i in range(2):
-            nc.vector.memset(e_in[i][:].bitcast(I32), 0)
-        nc.vector.memset(e_codes[:, C * ESLOT :].bitcast(I32), 0)
-        nc.vector.memset(e_scales[:, C * ESLOT :].bitcast(I32), 0)
+            words = a_in[i][:].bitcast(I32).rearrange("p (c w) -> p c w", c=XCH)
+            nc.vector.memset(words[:, :, AUSED * 2 :], 0)
         make_identity(nc, ident[:])
 
         piece_of = {}
@@ -144,38 +141,28 @@ def tile_conv2d_kernel(tc, x, weights, bias, grad_out, out):
                     load_x(i)
                 state["next"] = state["next"] + 1
 
-        a_in = {}
-
         def regroup(k):
             rows = x_tiles[k][:].rearrange("p (c w) -> p c w", c=XCH)[:, :, 0:RUN].rearrange(
                 "p c (d z) -> p c d z", d=KS
             )
-            at = apool.tile([P, XCH * P * 4], BF16, name="at", tag="at", align_bytes=64)
-            dst = at[:].rearrange("p (c s d t) -> p c s d t", c=XCH, d=KS, t=4)
+            dst = a_in[k % 2][:].rearrange("p (c s d t) -> p c s d t", c=XCH, d=KS, t=4)
             for d in range(KS):
                 nc.vector.tensor_copy(
-                    out=dst[:, :, :, d, :],
+                    out=dst[:, :, 0:32, d, :],
                     in_=rows[:, :, d, 0:P].rearrange("p c (t s) -> p c s t", t=4),
                 )
-            edst = e_in[k % 2][:].rearrange("p (c s d t) -> p c s d t", c=XCH, d=KS, t=4)
             for s in range(KS - 1):
-                nc.scalar.copy(out=edst[:, :, s, :, :], in_=rows[:, :, :, 32 + s : HW : 32])
-            a_in[k] = at
+                nc.scalar.copy(out=dst[:, :, 32 + s, :, :], in_=rows[:, :, :, 32 + s : HW : 32])
             state["x_done"] = k + 1
 
         def quantise_a(k):
-            w = XCH * P
-            nc.vector.quantize_mx(
-                out=a_codes[:, k * w : (k + 1) * w].bitcast(E4M3X4),
-                scales=a_scales[:, k * w : (k + 1) * w],
-                in_=a_in[k][:],
-            )
-            w = XCH * ESLOT
-            nc.vector.quantize_mx(
-                out=e_codes[:, k * w : (k + 1) * w].bitcast(E4M3X4),
-                scales=e_scales[:, k * w : (k + 1) * w],
-                in_=e_in[k % 2][:],
-            )
+            first = k * XCH * ACOL
+            for lo, hi in ((0, 512), (512, XCH * ACOL)):
+                nc.vector.quantize_mx(
+                    out=a_codes[:, first + lo : first + hi].bitcast(E4M3X4),
+                    scales=a_scales[:, first + lo : first + hi],
+                    in_=a_in[k % 2][:, 4 * lo : 4 * hi],
+                )
 
         def bank_words(c, h):
             i = piece_of[(c, h)]
@@ -238,8 +225,8 @@ def tile_conv2d_kernel(tc, x, weights, bias, grad_out, out):
             gc, gs = g_q[c]
             nc.tensor.matmul_mx(
                 out=r_main[:],
-                lhsT=a_codes[:, c * P : (c + 1) * P].bitcast(E4M3X4),
-                lhsT_scale=a_scales[:, c * P : (c + 1) * P],
+                lhsT=a_codes[:, c * ACOL : c * ACOL + P].bitcast(E4M3X4),
+                lhsT_scale=a_scales[:, c * ACOL : c * ACOL + P],
                 rhs=gc[:].bitcast(E5M2X4),
                 rhs_scale=gs[:],
                 start=(c == 0),
@@ -247,8 +234,8 @@ def tile_conv2d_kernel(tc, x, weights, bias, grad_out, out):
             )
             nc.tensor.matmul_mx(
                 out=r_extra[:],
-                lhsT=e_codes[:, c * ESLOT : c * ESLOT + P].bitcast(E4M3X4),
-                lhsT_scale=e_scales[:, c * ESLOT : c * ESLOT + P],
+                lhsT=a_codes[:, c * ACOL + 64 : c * ACOL + 64 + P].bitcast(E4M3X4),
+                lhsT_scale=a_scales[:, c * ACOL + 64 : c * ACOL + 64 + P],
                 rhs=gc[:].bitcast(E5M2X4),
                 rhs_scale=gs[:],
                 start=(c == 0),
@@ -282,7 +269,7 @@ def tile_conv2d_kernel(tc, x, weights, bias, grad_out, out):
                         sort_words(c, h)
             for i in range(2):
                 c = multiplied
-                if c < C and last_unit[c] < u and min(c + 1, C - 1) < quantised * XCH:
+                if c < C and last_unit[c] < u and c < quantised * XCH:
                     multiply(c)
                     multiplied += 1
             u += 1
@@ -290,12 +277,9 @@ def tile_conv2d_kernel(tc, x, weights, bias, grad_out, out):
         main_sb = keep.tile([P, CO], F32, name="main_sb")
         extra_sb = keep.tile([P, CO], F32, name="extra_sb")
         nc.vector.tensor_copy(out=main_sb[:], in_=r_main[:])
-        nc.scalar.copy(out=extra_sb[0:16, :], in_=r_extra[0:16, :])
+        nc.scalar.copy(out=extra_sb[:], in_=r_extra[:])
         nc.sync.dma_start(out=out_v[0, :, :], in_=main_sb[:, :])
-        nc.scalar.dma_start(out=out_v[2, 8:120, :], in_=main_sb[16:P, :])
-        nc.sync.dma_start(out=out_v[1, 12:124, :], in_=main_sb[16:P, :])
-        nc.scalar.dma_start(out=out_v[3, 4:116, :], in_=main_sb[16:P, :])
         for j in range(1, KS):
-            eng = nc.sync if j % 2 == 1 else nc.scalar
-            eng.dma_start(out=out_v[j, 0 : 16 - 4 * j, :], in_=main_sb[4 * j : 16, :])
-            eng.dma_start(out=out_v[j, P - 4 * j : P, :], in_=extra_sb[0 : 4 * j, :])
+            eng = nc.sync if j == 1 else nc.scalar
+            eng.dma_start(out=out_v[j, 0:64, :], in_=main_sb[4 * j : 4 * j + 64, :])
+            eng.dma_start(out=out_v[j, 64:P, :], in_=extra_sb[4 * j : 4 * j + 64, :])

@@ -19,7 +19,7 @@ CO = 512
 TOK = 512
 WORDS = TOK // 2
 RUN = KS * HW
-PITCH = 528
+PITCH = 560
 XCH = 4
 NXC = C // XCH
 ACOL = 192
@@ -142,17 +142,20 @@ def tile_conv2d_kernel(tc, x, weights, bias, grad_out, out):
                 state["next"] = state["next"] + 1
 
         def regroup(k):
-            rows = x_tiles[k][:].rearrange("p (c w) -> p c w", c=XCH)[:, :, 0:RUN].rearrange(
-                "p c (d z) -> p c d z", d=KS
+            runs = x_tiles[k][:].rearrange("p (c w) -> p c w", c=XCH)
+            dst = a_in[k % 2][:].rearrange("p (c s d t) -> p c d s t", c=XCH, d=KS, t=4)
+            nc.vector.tensor_copy(
+                out=dst[:, :, :, 0:32, :],
+                in_=runs[:, :, 0:RUN]
+                .rearrange("p c (d z) -> p c d z", d=KS)[:, :, :, 0:P]
+                .rearrange("p c d (t s) -> p c d s t", t=4),
             )
-            dst = a_in[k % 2][:].rearrange("p (c s d t) -> p c s d t", c=XCH, d=KS, t=4)
-            for d in range(KS):
-                nc.vector.tensor_copy(
-                    out=dst[:, :, 0:32, d, :],
-                    in_=rows[:, :, d, 0:P].rearrange("p c (t s) -> p c s t", t=4),
-                )
-            for s in range(KS - 1):
-                nc.scalar.copy(out=dst[:, :, 32 + s, :, :], in_=rows[:, :, :, 32 + s : HW : 32])
+            nc.scalar.copy(
+                out=dst[:, :, :, 32:35, :],
+                in_=runs[:, :, 32 : 32 + RUN]
+                .rearrange("p c (d z) -> p c d z", d=KS)[:, :, :, 0:P]
+                .rearrange("p c d (t s) -> p c d s t", t=4)[:, :, :, 0:3, :],
+            )
             state["x_done"] = k + 1
 
         def quantise_a(k):

@@ -61,7 +61,7 @@ def tile_conv2d_kernel(tc, x, weights, bias, grad_out, out):
         gpool = ctx.enter_context(tc.tile_pool(name="gload", bufs=G_BUFS))
         xpool = ctx.enter_context(tc.tile_pool(name="xload", bufs=X_BUFS))
         qpool = ctx.enter_context(tc.tile_pool(name="ggroup", bufs=8))
-        cpool = ctx.enter_context(tc.tile_pool(name="gcodes", bufs=8))
+        cpool = ctx.enter_context(tc.tile_pool(name="gcodes", bufs=14))
         spool = ctx.enter_context(tc.tile_pool(name="gsort", bufs=8))
         psum_t = ctx.enter_context(tc.psum_pool(name="psum_t", bufs=6))
         psum_r = ctx.enter_context(tc.psum_pool(name="psum_r", bufs=1))
@@ -245,6 +245,12 @@ def tile_conv2d_kernel(tc, x, weights, bias, grad_out, out):
                 stop=(c == C - 1),
             )
 
+        def multiply_next(c, newest_unit, chunks_ready):
+            if c < C and last_unit[c] <= newest_unit and c < chunks_ready * XCH:
+                multiply(c)
+                return 1
+            return 0
+
         pump()
         regroup(0)
         pump()
@@ -255,7 +261,9 @@ def tile_conv2d_kernel(tc, x, weights, bias, grad_out, out):
         u = 0
         while multiplied < C:
             if u < len(units):
-                transpose_and_copy(units[u])
+                transpose_and_copy(units[u][0:2])
+                multiplied += multiply_next(multiplied, u - 2, quantised)
+                transpose_and_copy(units[u][2:4])
                 pump()
             if 0 < u <= len(units):
                 quantise_g(units[u - 1])
@@ -270,11 +278,11 @@ def tile_conv2d_kernel(tc, x, weights, bias, grad_out, out):
                 for c, h in units[u + 1]:
                     if is_sorted(c):
                         sort_words(c, h)
-            for i in range(2):
-                c = multiplied
-                if c < C and last_unit[c] < u and c < quantised * XCH:
-                    multiply(c)
-                    multiplied += 1
+            if u + 1 < len(units):
+                multiplied += multiply_next(multiplied, u - 2, quantised)
+            else:
+                for i in range(C):
+                    multiplied += multiply_next(multiplied, u - 1, quantised)
             u += 1
 
         main_sb = keep.tile([P, CO], F32, name="main_sb")

from contextlib import ExitStack

import concourse.mybir as mybir
from concourse.masks import make_identity

BF16 = mybir.dt.bfloat16
F32 = mybir.dt.float32
I32 = mybir.dt.int32
U32 = mybir.dt.uint32
U8 = mybir.dt.uint8
E4M3X4 = mybir.dt.float8_e4m3fn_x4
E5M2X4 = mybir.dt.float8_e5m2_x4

P = 128
C = 32
HW = 131
KS = 4
CO = 512
TOK = 512
WORDS = TOK // 2
RUN = KS * HW
PITCH = 560
XCH = 4
NXC = C // XCH
ACOL = 192
AUSED = 140
G_BUFS = 9
X_BUFS = 4
FLOPS = 2 * C * TOK * 512 * CO


def pair_unit(c):
    return ((c, 0), (c, 1), (c + 1, 0), (c + 1, 1))


def g_plan():
    pieces = [(0, 1, 0, 1), (0, 1, 1, 1), (1, 1, 0, 2)]
    units = [pair_unit(0)]
    for c in (2, 4, 6):
        pieces.append((c, 2, 0, 2))
        units.append(pair_unit(c))
    for c in range(8, 28, 4):
        for h in range(2):
            pieces.append((c, 4, h, 1))
            units.append(tuple((c + i, h) for i in range(4)))
    for c in (28, 30):
        pieces.append((c, 2, 0, 2))
        units.append(pair_unit(c))
    return pieces, units


def is_sorted(c):
    return (c >= 24 and c % 2 == 1) or (c >= 12 and c % 4 == 3)


def tile_conv2d_kernel(tc, x, weights, bias, grad_out, out):
    nc = tc.nc
    pieces, units = g_plan()
    with ExitStack() as ctx:
        keep = ctx.enter_context(tc.tile_pool(name="keep", bufs=1))
        gpool = ctx.enter_context(tc.tile_pool(name="gload", bufs=G_BUFS))
        xpool = ctx.enter_context(tc.tile_pool(name="xload", bufs=X_BUFS))
        qpool = ctx.enter_context(tc.tile_pool(name="ggroup", bufs=8))
        cpool = ctx.enter_context(tc.tile_pool(name="gcodes", bufs=14))
        spool = ctx.enter_context(tc.tile_pool(name="gsort", bufs=8))
        psum_t = ctx.enter_context(tc.psum_pool(name="psum_t", bufs=6))
        psum_r = ctx.enter_context(tc.psum_pool(name="psum_r", bufs=1))
        ctx.enter_context(tc.manual_schedule())

        x_v = x.rearrange("n c y z -> (n c) y z")
        g_v = grad_out.rearrange("n (j p) u v -> p (n j) (u v)", p=P)
        out_v = out.rearrange("(m j) o -> j m o", j=KS)

        ident = keep.tile([P, P], F32, name="ident")
        a_codes = keep.tile([P, C * ACOL], U32, name="a_codes", align_bytes=64)
        a_scales = keep.tile([P, C * ACOL], U8, name="a_scales", align_bytes=64)
        a_in = [
            keep.tile([P, XCH * ACOL * 4], BF16, name="a_in%d" % i, align_bytes=64)
            for i in range(2)
        ]
        r_main = psum_r.tile([P, CO], F32, name="r_main")
        r_extra = psum_r.tile([P, CO], F32, name="r_extra")

        for i in range(2):
            words = a_in[i][:].bitcast(I32).rearrange("p (c w) -> p c w", c=XCH)
            nc.vector.memset(words[:, :, AUSED * 2 :], 0)
        make_identity(nc, ident[:])

        piece_of = {}
        for i, (c0, n, h0, nh) in enumerate(pieces):
            for c in range(c0, c0 + n):
                for h in range(h0, h0 + nh):
                    piece_of[(c, h)] = i
        last_unit = {}
        for u, unit in enumerate(units):
            for c, h in unit:
                last_unit[c] = u

        plan = []
        for i, (c0, n, h0, nh) in enumerate(pieces):
            if c0 % XCH == 0 and h0 == 0 and c0 > 0:
                plan.append(("x", c0 // XCH))
            plan.append(("g", i))
            if i == 1:
                plan.append(("x", 0))
        g_tiles = {}
        x_tiles = {}
        banks_left = [n * nh for (c0, n, h0, nh) in pieces]
        state = {"next": 0, "x_done": 0}

        def load_g(i):
            c0, n, h0, nh = pieces[i]
            gt = gpool.tile([P, 2 * nh * n * TOK], BF16, name="gt", tag="gt")
            nc.sync.dma_start(
                out=gt[:].rearrange("p (j r) -> p j r", j=2 * nh),
                in_=g_v[:, 2 * h0 : 2 * (h0 + nh), c0 * TOK : (c0 + n) * TOK],
            )
            g_tiles[i] = gt

        def load_x(k):
            xt = xpool.tile([P, XCH * PITCH], BF16, name="xt", tag="xt")
            for b in range(KS):
                nc.sync.dma_start(
                    out=xt[b:P:KS, :].rearrange("a (c w) -> a c w", c=XCH)[:, :, 0:RUN],
                    in_=x_v[k * XCH : (k + 1) * XCH, b : b + P, :].rearrange(
                        "c (a r) z -> a c (r z)", r=KS
                    ),
                )
            x_tiles[k] = xt

        def pump():
            while state["next"] < len(plan):
                kind, i = plan[state["next"]]
                if kind == "g" and i >= G_BUFS and banks_left[i - G_BUFS] > 0:
                    return
                if kind == "x" and i >= X_BUFS and state["x_done"] < i - X_BUFS + 1:
                    return
                if kind == "g":
                    load_g(i)
                else:
                    load_x(i)
                state["next"] = state["next"] + 1

        def regroup(k):
            runs = x_tiles[k][:].rearrange("p (c w) -> p c w", c=XCH)
            dst = a_in[k % 2][:].rearrange("p (c s d t) -> p c d s t", c=XCH, d=KS, t=4)
            nc.vector.tensor_copy(
                out=dst[:, :, :, 0:32, :],
                in_=runs[:, :, 0:RUN]
                .rearrange("p c (d z) -> p c d z", d=KS)[:, :, :, 0:P]
                .rearrange("p c d (t s) -> p c d s t", t=4),
            )
            nc.scalar.copy(
                out=dst[:, :, :, 32:35, :],
                in_=runs[:, :, 32 : 32 + RUN]
                .rearrange("p c (d z) -> p c d z", d=KS)[:, :, :, 0:P]
                .rearrange("p c d (t s) -> p c d s t", t=4)[:, :, :, 0:3, :],
            )
            state["x_done"] = k + 1

        def quantise_a(k):
            first = k * XCH * ACOL
            for lo, hi in ((0, 512), (512, XCH * ACOL)):
                nc.vector.quantize_mx(
                    out=a_codes[:, first + lo : first + hi].bitcast(E4M3X4),
                    scales=a_scales[:, first + lo : first + hi],
                    in_=a_in[k % 2][:, 4 * lo : 4 * hi],
                )

        def bank_words(c, h):
            i = piece_of[(c, h)]
            c0, n, h0, nh = pieces[i]
            words = g_tiles[i][:].bitcast(F32).rearrange("p (j r) -> p j r", j=2 * nh)
            return words[:, 2 * (h - h0) : 2 * (h - h0) + 2, (c - c0) * WORDS : (c - c0 + 1) * WORDS]

        sorted_words = {}

        def sort_words(c, h):
            st = spool.tile([P, 2 * WORDS], F32, name="st", tag="st")
            nc.vector.tensor_copy(
                out=st[:].rearrange("p (j u i) -> p j u i", j=2, u=2),
                in_=bank_words(c, h).rearrange("p j (i u) -> p j u i", u=2),
            )
            sorted_words[(c, h)] = st

        grouped = {}

        def transpose_and_copy(unit):
            banks = []
            for c, h in unit:
                pt = psum_t.tile([P, 2, 256], F32, name="pt", tag="pt")
                for jj in range(2):
                    for u in range(2):
                        if is_sorted(c):
                            first = (jj * 2 + u) * P
                            src = sorted_words[(c, h)][:, first : first + P]
                        else:
                            src = bank_words(c, h)[:, jj, u:WORDS:2]
                        nc.tensor.transpose(
                            out=pt[:, u, jj * P : (jj + 1) * P], in_=src, identity=ident[:]
                        )
                banks.append(pt)
                banks_left[piece_of[(c, h)]] -= 1
            for (c, h), pt in zip(unit, banks):
                gq = qpool.tile([P, 1024], BF16, name="gq", tag="gq", align_bytes=64)
                nc.scalar.copy(
                    out=gq[:].bitcast(F32).rearrange("p (o u) -> p o u", u=2),
                    in_=pt[:].rearrange("p u o -> p o u"),
                )
                grouped[(c, h)] = gq

        g_q = {}

        def quantise_g(unit):
            for c, h in unit:
                if c not in g_q:
                    gc = cpool.tile([P, CO], U32, name="gc", tag="gc", align_bytes=64)
                    gs = cpool.tile([P, CO], U8, name="gs", tag="gs", align_bytes=64)
                    g_q[c] = (gc, gs)
                gc, gs = g_q[c]
                nc.vector.quantize_mx(
                    out=gc[:, h * 256 : (h + 1) * 256].bitcast(E5M2X4),
                    scales=gs[:, h * 256 : (h + 1) * 256],
                    in_=grouped[(c, h)][:],
                )

        def multiply(c):
            gc, gs = g_q[c]
            nc.tensor.matmul_mx(
                out=r_main[:],
                lhsT=a_codes[:, c * ACOL : c * ACOL + P].bitcast(E4M3X4),
                lhsT_scale=a_scales[:, c * ACOL : c * ACOL + P],
                rhs=gc[:].bitcast(E5M2X4),
                rhs_scale=gs[:],
                start=(c == 0),
                stop=(c == C - 1),
            )
            nc.tensor.matmul_mx(
                out=r_extra[:],
                lhsT=a_codes[:, c * ACOL + 64 : c * ACOL + 64 + P].bitcast(E4M3X4),
                lhsT_scale=a_scales[:, c * ACOL + 64 : c * ACOL + 64 + P],
                rhs=gc[:].bitcast(E5M2X4),
                rhs_scale=gs[:],
                start=(c == 0),
                stop=(c == C - 1),
            )

        def multiply_next(c, newest_unit, chunks_ready):
            if c < C and last_unit[c] <= newest_unit and c < chunks_ready * XCH:
                multiply(c)
                return 1
            return 0

        pump()
        regroup(0)
        pump()
        quantise_a(0)
        regrouped = 1
        quantised = 1
        multiplied = 0
        u = 0
        while multiplied < C:
            if u < len(units):
                transpose_and_copy(units[u][0:2])
                multiplied += multiply_next(multiplied, u - 2, quantised)
                transpose_and_copy(units[u][2:4])
                pump()
            if 0 < u <= len(units):
                quantise_g(units[u - 1])
            if quantised < regrouped and u > last_unit[quantised * XCH - 1]:
                quantise_a(quantised)
                quantised += 1
            if regrouped < NXC and u >= last_unit[regrouped * XCH - 1]:
                regroup(regrouped)
                regrouped += 1
                pump()
            if u + 1 < len(units):
                for c, h in units[u + 1]:
                    if is_sorted(c):
                        sort_words(c, h)
            if u + 1 < len(units):
                multiplied += multiply_next(multiplied, u - 2, quantised)
            else:
                for i in range(C):
                    multiplied += multiply_next(multiplied, u - 1, quantised)
            u += 1

        main_sb = keep.tile([P, CO], F32, name="main_sb")
        extra_sb = keep.tile([P, CO], F32, name="extra_sb")
        nc.vector.tensor_copy(out=main_sb[:], in_=r_main[:])
        nc.scalar.copy(out=extra_sb[:], in_=r_extra[:])
        nc.sync.dma_start(out=out_v[0, :, :], in_=main_sb[:, :])
        for j in range(1, KS):
            eng = nc.sync if j == 1 else nc.scalar
            eng.dma_start(out=out_v[j, 0:64, :], in_=main_sb[4 * j : 4 * j + 64, :])
            eng.dma_start(out=out_v[j, 64:P, :], in_=extra_sb[4 * j : 4 * j + 64, :])
